import numpy as np
import ml_dtypes


def mxq(x, axis, fmt="e4m3"):
    dtype, down = {"e4m3": (ml_dtypes.float8_e4m3fn, 7), "e5m2": (ml_dtypes.float8_e5m2, 14)}[fmt]
    v = np.moveaxis(np.asarray(x, np.float32).astype(ml_dtypes.bfloat16).astype(np.float64), axis, -1)
    blocks = v.reshape(v.shape[:-1] + (-1, 32))
    amax = np.abs(blocks).max(-1, keepdims=True)
    byte = np.maximum(np.where(amax > 0, np.frexp(amax)[1] - 1 + 127, 0) - down, 1)
    scale = np.exp2(byte - 127.0)
    codes = (blocks / scale).astype(np.float32).astype(dtype).astype(np.float64)
    return np.moveaxis((codes * scale).reshape(v.shape), -1, axis)


WIDE = False


def mx_kscale(k):
    if not WIDE:
        return np.ones(k)
    levels = np.array([10, -10, 5, -5, 0])
    a = np.random.permutation(np.resize(levels, k // 512 * 4)).reshape(k // 512, 4)
    idx = np.arange(k)
    return np.exp2(a[idx // 512, idx % 128 // 32])


BF16 = ml_dtypes.bfloat16


def bf(x):
    return np.asarray(x, np.float32).astype(BF16)


def f64(x):
    return np.asarray(x).astype(np.float64)


E2M1 = np.array([0.0, 0.5, 1.0, 1.5, 2.0, 3.0, 4.0, 6.0, -0.0, -0.5, -1.0, -1.5, -2.0, -3.0, -4.0, -6.0])


def pack_weight(w, fmt):
    k, n = w.shape
    w = f64(bf(w)).reshape(k // 32, 32, n)
    amax = np.abs(w).max(1)
    if fmt == "e4m3":
        byte = np.frexp(amax)[1] - 1 + 127 - 7
    else:
        mant, ex = np.frexp(amax / 6.0)
        byte = np.where(mant > 0.5, ex, ex - 1) + 127
    byte = np.clip(np.where(amax > 0, byte, 1), 1, 254)
    scaled = (w * np.exp2(127.0 - byte)[:, None, :]).reshape(k, n).astype(np.float32)
    by_word = np.ascontiguousarray(scaled.reshape(k // 512, 128, 4, n).transpose(0, 1, 3, 2))
    if fmt == "e4m3":
        words = by_word.astype(ml_dtypes.float8_e4m3fn).view(np.uint8)
    else:
        c = by_word.astype(ml_dtypes.float4_e2m1fn).view(np.uint8) & 0xF
        words = c[..., 0::2] | (c[..., 1::2] << 4)
    return np.ascontiguousarray(words), np.ascontiguousarray(byte.astype(np.uint8).reshape(k // 512, 16, n))


def unpack_weight(words, scales, fmt):
    g, p, n, _ = words.shape
    if fmt == "e4m3":
        vals = np.ascontiguousarray(words).view(ml_dtypes.float8_e4m3fn).astype(np.float64)
    else:
        nib = np.empty((g, p, n, 4), np.uint8)
        nib[..., 0::2] = words & 0xF
        nib[..., 1::2] = words >> 4
        vals = E2M1[nib]
    vals = vals * np.repeat(np.exp2(scales.astype(np.float64) - 127.0), 8, axis=1)[..., None]
    return vals.transpose(0, 1, 3, 2).reshape(g * 512, n)


B, STOCH, ACT_DIM, HIDDEN, DETER = 8192, 384, 128, 512, 128
K1 = STOCH + ACT_DIM
EPS = 1e-4
FMT = "e4m3"


def silu(v):
    return v / (1.0 + np.exp(-v))


def rmsnorm(v, w):
    return v * (1.0 / np.sqrt(np.mean(v * v, axis=-1, keepdims=True) + EPS)) * w


def setup_inputs():
    s = mx_kscale(K1)[:STOCH]
    w1 = np.random.standard_normal((HIDDEN, K1)) * 0.07 / np.sqrt(K1)
    w1[:, :STOCH] = w1[:, :STOCH] / s
    stoch = bf(np.random.standard_normal((B, STOCH)) * s)
    action = bf(np.random.standard_normal((B, ACT_DIM)))
    w1_words, w1_scales = pack_weight(np.ascontiguousarray(w1.T), FMT)
    tok_b1 = bf(np.random.standard_normal(HIDDEN) * 0.03)
    tok_nw = bf(1.0 + 0.1 * np.random.standard_normal(HIDDEN))
    w2 = np.random.standard_normal((DETER, HIDDEN)) * 1.5 / np.sqrt(HIDDEN)
    w2_words, w2_scales = pack_weight(np.ascontiguousarray(w2.T), FMT)
    tok_b2 = bf(np.random.standard_normal(DETER) * 0.2)
    return {"stoch": stoch,
            "action": action,
            "tok_w1_words": w1_words,
            "tok_w1_scales": w1_scales,
            "tok_b1": tok_b1,
            "tok_nw": tok_nw,
            "tok_w2_words": w2_words,
            "tok_w2_scales": w2_scales,
            "tok_b2": tok_b2}


def reference(stoch, action, tok_w1_words, tok_w1_scales, tok_b1, tok_nw, tok_w2_words, tok_w2_scales, tok_b2):
    act = f64(action)
    act = act / np.maximum(np.abs(act), 1.0)
    u = np.concatenate([f64(stoch), act], axis=-1)
    h = (mxq(u, 1, "e4m3") @ unpack_weight(tok_w1_words, tok_w1_scales, FMT)) + f64(tok_b1)
    g = silu(rmsnorm(h, f64(tok_nw)))
    return (mxq(g, 1, "e4m3") @ unpack_weight(tok_w2_words, tok_w2_scales, FMT)) + f64(tok_b2)

@@ -1,0 +1,266 @@
+from contextlib import ExitStack
+
+import concourse.mybir as mybir
+from concourse.masks import make_identity
+
+F32 = mybir.dt.float32
+BF16 = mybir.dt.bfloat16
+I32 = mybir.dt.int32
+U32 = mybir.dt.uint32
+U8 = mybir.dt.uint8
+FP8X4 = mybir.dt.float8_e4m3fn_x4
+ALU = mybir.AluOpType
+ACT = mybir.ActivationFunctionType
+
+P = 128
+PACK = 4
+TOKENS = 8192
+STOCH = 384
+ACT_DIM = 128
+K1 = STOCH + ACT_DIM
+HIDDEN = 512
+DETER = 128
+EPS = 1e-4
+
+TILES_PER_GROUP = 4
+GROUP_TOKENS = P * TILES_PER_GROUP
+N_GROUPS = TOKENS // GROUP_TOKENS
+
+FLOPS = 2 * TOKENS * K1 * HIDDEN + 2 * TOKENS * HIDDEN * DETER
+
+
+def tile_mamba2backbone_pa_t_kernel(
+    tc,
+    stoch,
+    action,
+    tok_w1_words,
+    tok_w1_scales,
+    tok_b1,
+    tok_nw,
+    tok_w2_words,
+    tok_w2_scales,
+    tok_b2,
+    out,
+):
+    nc = tc.nc
+
+    stoch_groups = stoch.rearrange("(g p j) k -> g p j k", p=P, j=TILES_PER_GROUP)
+    action_groups = action.rearrange("(g p j) k -> g p j k", p=P, j=TILES_PER_GROUP)
+    out_groups = out.rearrange("(g p j) n -> g p j n", p=P, j=TILES_PER_GROUP)
+
+    with ExitStack() as ctx:
+        const = ctx.enter_context(tc.tile_pool(name="const", bufs=1))
+        inputs = ctx.enter_context(tc.tile_pool(name="inputs", bufs=N_GROUPS))
+        per_group = ctx.enter_context(tc.tile_pool(name="per_group", bufs=3))
+        per_tile = ctx.enter_context(tc.tile_pool(name="per_tile", bufs=2 * TILES_PER_GROUP))
+        psum_u = ctx.enter_context(tc.psum_pool(name="psum_u", bufs=2))
+        psum_h = ctx.enter_context(tc.psum_pool(name="psum_h", bufs=2))
+        psum_z = ctx.enter_context(tc.psum_pool(name="psum_z", bufs=3))
+        psum_o = ctx.enter_context(tc.psum_pool(name="psum_o", bufs=1))
+        ctx.enter_context(tc.manual_schedule())
+
+        held = {}
+
+        def load_group(g):
+            u_rows = inputs.tile([P, TILES_PER_GROUP, K1], BF16)
+            nc.sync.dma_start(out=u_rows[:, :, STOCH:K1], in_=action_groups[g])
+            nc.sync.dma_start(out=u_rows[:, :, 0:STOCH], in_=stoch_groups[g])
+            held["u_rows", g] = u_rows
+
+        def load_weight(words_dram, scales_dram, words, plane):
+            nc.sync.dma_start(
+                out=words[:].bitcast(I32),
+                in_=words_dram[0].rearrange("p n t -> p (n t)").bitcast(I32),
+            )
+            for quadrant in range(4):
+                nc.sync.dma_start(
+                    out=plane[32 * quadrant : 32 * quadrant + 4, :].bitcast(I32),
+                    in_=scales_dram[0, 4 * quadrant : 4 * quadrant + 4, :].bitcast(I32),
+                )
+
+        w1_words = const.tile([P, PACK * HIDDEN], U8, align_bytes=64)
+        w1_plane = const.tile([P, HIDDEN], U8, align_bytes=64)
+        w2_words = const.tile([P, PACK * DETER], U8, align_bytes=64)
+        w2_plane = const.tile([P, DETER], U8, align_bytes=64)
+        nc.vector.memset(w1_plane[:].bitcast(I32), 0)
+        nc.vector.memset(w2_plane[:].bitcast(I32), 0)
+
+        load_group(0)
+        load_weight(tok_w1_words, tok_w1_scales, w1_words, w1_plane)
+        load_group(1)
+        load_weight(tok_w2_words, tok_w2_scales, w2_words, w2_plane)
+        for g in range(2, N_GROUPS):
+            load_group(g)
+
+        b1_rows = const.tile([P, HIDDEN], BF16)
+        nw_rows = const.tile([P, HIDDEN], BF16)
+        b2_rows = const.tile([P, DETER], BF16)
+        nc.scalar.dma_start(out=b1_rows[:], in_=tok_b1.partition_broadcast(P))
+        nc.scalar.dma_start(out=nw_rows[:], in_=tok_nw.partition_broadcast(P))
+        nc.scalar.dma_start(out=b2_rows[:], in_=tok_b2.partition_broadcast(P))
+
+        warm = const.tile([P, 1], F32)
+        nc.vector.memset(warm[:], 0.0)
+        nc.scalar.activation(out=warm[:], in_=warm[:], func=ACT.Silu)
+
+        identity = const.tile([P, P], F32)
+        make_identity(nc, identity[:])
+        minus_half = const.tile([P, TILES_PER_GROUP], F32)
+        nc.gpsimd.memset(minus_half[:], -0.5)
+
+        def clamp_action(g):
+            an = held["u_rows", g][:, :, STOCH:K1]
+            nc.vector.tensor_scalar(out=an, in0=an, scalar1=1.0, scalar2=-1.0, op0=ALU.min, op1=ALU.max)
+
+        clamp_action(0)
+
+        b1_sorted = const.tile([P, PACK, P], F32)
+        nw_sorted = const.tile([P, PACK, P], F32)
+        b2_f32 = const.tile([P, DETER], F32)
+        nc.vector.tensor_copy(out=b1_sorted[:], in_=b1_rows[:].rearrange("p (q t) -> p t q", t=PACK))
+        nc.vector.tensor_copy(out=nw_sorted[:], in_=nw_rows[:].rearrange("p (q t) -> p t q", t=PACK))
+        nc.vector.tensor_copy(out=b2_f32[:], in_=b2_rows[:])
+
+        def transpose_u(g):
+            u_rows = held["u_rows", g]
+            for pair in range(TILES_PER_GROUP // 2):
+                u_bank = psum_u.tile([P, 2, 2, P], F32)
+                for i in range(2):
+                    words = u_rows[:, 2 * pair + i, :].bitcast(F32)
+                    for half in range(2):
+                        nc.tensor.transpose(u_bank[:, i, half, :], words[:, half : K1 // 2 : 2], identity[:])
+                held["u_bank", g, pair] = u_bank
+
+        def copy_u(g):
+            u_grouped = per_group.tile([P, PACK * GROUP_TOKENS], BF16, align_bytes=64)
+            as_words = u_grouped[:].bitcast(F32).rearrange("p (r i w h) -> p r i w h", r=2, i=2, h=2)
+            for pair in range(TILES_PER_GROUP // 2):
+                nc.scalar.copy(
+                    out=as_words[:, pair],
+                    in_=held["u_bank", g, pair][:].rearrange("p i h w -> p i w h"),
+                )
+            held["u_grouped", g] = u_grouped
+
+        def quantise(name, g):
+            grouped = held[name + "_grouped", g]
+            codes = per_group.tile([P, GROUP_TOKENS], U32, align_bytes=64, tag=name + "_codes")
+            scales = per_group.tile([P, GROUP_TOKENS], U8, align_bytes=64, tag=name + "_scales")
+            nc.vector.quantize_mx(out=codes[:].bitcast(FP8X4), scales=scales[:], in_=grouped[:])
+            held[name + "_codes", g] = codes
+            held[name + "_scales", g] = scales
+
+        def first_matmul(g, j):
+            tokens = slice(P * j, P * (j + 1))
+            h_bank = psum_h.tile([P, HIDDEN], F32)
+            nc.tensor.matmul_mx(
+                out=h_bank[:],
+                lhsT=held["u_codes", g][:, tokens].bitcast(FP8X4),
+                lhsT_scale=held["u_scales", g][:, tokens],
+                rhs=w1_words[:].bitcast(FP8X4),
+                rhs_scale=w1_plane[:],
+                start=True,
+                stop=True,
+            )
+            held["h_bank", g, j] = h_bank
+
+        def add_bias_and_square(g, j):
+            if j == 0:
+                sum_sq = per_group.tile([P, TILES_PER_GROUP], F32)
+                held["sum_sq", g] = sum_sq
+            h_sorted = per_tile.tile([P, PACK, P], F32)
+            nc.vector.tensor_tensor(
+                out=h_sorted[:],
+                in0=held["h_bank", g, j][:].rearrange("p (q t) -> p t q", t=PACK),
+                in1=b1_sorted[:],
+                op=ALU.add,
+            )
+            squares = per_tile.tile([P, PACK, P], BF16)
+            nc.scalar.activation(
+                out=squares[:], in_=h_sorted[:], func=ACT.Square, accum_out=held["sum_sq", g][:, j : j + 1]
+            )
+            held["h_sorted", g, j] = h_sorted
+
+        def inverse_rms(g):
+            mean_sq = per_group.tile([P, TILES_PER_GROUP], F32)
+            inv_rms = per_group.tile([P, TILES_PER_GROUP], F32)
+            nc.gpsimd.tensor_scalar(
+                out=mean_sq[:], in0=held["sum_sq", g][:], scalar1=1.0 / HIDDEN, scalar2=EPS, op0=ALU.mult, op1=ALU.add
+            )
+            nc.gpsimd.tensor_tensor(out=inv_rms[:], in0=mean_sq[:], in1=minus_half[:], op=ALU.pow)
+            held["inv_rms", g] = inv_rms
+
+        def normalise_transpose_silu(g, j):
+            if j == 0:
+                g_grouped = per_group.tile([P, PACK * GROUP_TOKENS], BF16, align_bytes=64)
+                held["g_grouped", g] = g_grouped
+            z_sorted = per_tile.tile([P, PACK, P], F32)
+            nc.vector.scalar_tensor_tensor(
+                out=z_sorted[:],
+                in0=held["h_sorted", g, j][:],
+                scalar=held["inv_rms", g][:, j : j + 1],
+                in1=nw_sorted[:],
+                op0=ALU.mult,
+                op1=ALU.mult,
+            )
+            z_bank = psum_z.tile([P, PACK, P], F32)
+            for t in range(PACK):
+                nc.tensor.transpose(z_bank[:, t, :], z_sorted[:, t, :], identity[:])
+            nc.scalar.activation(
+                out=held["g_grouped", g][:, PACK * P * j : PACK * P * (j + 1)].rearrange("p (w t) -> p w t", t=PACK),
+                in_=z_bank[:].rearrange("p t w -> p w t"),
+                func=ACT.Silu,
+            )
+
+        def second_matmul(g):
+            o_bank = psum_o.tile([P, TILES_PER_GROUP, DETER], F32)
+            for j in range(TILES_PER_GROUP):
+                tokens = slice(P * j, P * (j + 1))
+                nc.tensor.matmul_mx(
+                    out=o_bank[:, j, :],
+                    lhsT=held["g_codes", g][:, tokens].bitcast(FP8X4),
+                    lhsT_scale=held["g_scales", g][:, tokens],
+                    rhs=w2_words[:].bitcast(FP8X4),
+                    rhs_scale=w2_plane[:],
+                    start=True,
+                    stop=True,
+                )
+            held["o_bank", g] = o_bank
+
+        def add_bias_and_store(g):
+            o_rows = per_group.tile([P, TILES_PER_GROUP, DETER], F32)
+            nc.vector.tensor_tensor(
+                out=o_rows[:],
+                in0=held["o_bank", g][:],
+                in1=b2_f32[:].unsqueeze(1).to_broadcast([P, TILES_PER_GROUP, DETER]),
+                op=ALU.add,
+            )
+            nc.sync.dma_start(out=out_groups[g], in_=o_rows[:])
+
+        def is_group(g):
+            return 0 <= g < N_GROUPS
+
+        for s in range(-2, N_GROUPS + 2):
+            if is_group(s + 1):
+                copy_u(s + 1)
+            if is_group(s):
+                for j in range(TILES_PER_GROUP):
+                    add_bias_and_square(s, j)
+                    if j + 2 < TILES_PER_GROUP:
+                        first_matmul(s, j + 2)
+                inverse_rms(s)
+            if is_group(s + 3):
+                clamp_action(s + 3)
+            if is_group(s + 2):
+                transpose_u(s + 2)
+            if is_group(s + 1):
+                quantise("u", s + 1)
+                first_matmul(s + 1, 0)
+                first_matmul(s + 1, 1)
+            if is_group(s - 2):
+                quantise("g", s - 2)
+                second_matmul(s - 2)
+            if is_group(s - 1):
+                for j in range(TILES_PER_GROUP):
+                    normalise_transpose_silu(s - 1, j)
+            if is_group(s - 2):
+                add_bias_and_store(s - 2)

@@ -24,7 +24,14 @@ EPS = 1e-4
 
 TILES_PER_GROUP = 4
 GROUP_TOKENS = P * TILES_PER_GROUP
+N_TILES = TOKENS // P
 N_GROUPS = TOKENS // GROUP_TOKENS
+
+U_AHEAD = 10
+H_AHEAD = 2
+NORM_LAG = 4
+
+FIRST_MATMUL_PASSES = 2
 
 FLOPS = 2 * TOKENS * K1 * HIDDEN + 2 * TOKENS * HIDDEN * DETER
 
@@ -52,9 +59,9 @@ def tile_mamba2backbone_pa_t_kernel(
         const = ctx.enter_context(tc.tile_pool(name="const", bufs=1))
         inputs = ctx.enter_context(tc.tile_pool(name="inputs", bufs=N_GROUPS))
         per_group = ctx.enter_context(tc.tile_pool(name="per_group", bufs=3))
-        per_tile = ctx.enter_context(tc.tile_pool(name="per_tile", bufs=2 * TILES_PER_GROUP))
+        per_tile = ctx.enter_context(tc.tile_pool(name="per_tile", bufs=NORM_LAG + 2))
         psum_u = ctx.enter_context(tc.psum_pool(name="psum_u", bufs=2))
-        psum_h = ctx.enter_context(tc.psum_pool(name="psum_h", bufs=2))
+        psum_h = ctx.enter_context(tc.psum_pool(name="psum_h", bufs=H_AHEAD))
         psum_z = ctx.enter_context(tc.psum_pool(name="psum_z", bufs=3))
         psum_o = ctx.enter_context(tc.psum_pool(name="psum_o", bufs=1))
         ctx.enter_context(tc.manual_schedule())
@@ -88,8 +95,9 @@ def tile_mamba2backbone_pa_t_kernel(
         load_group(0)
         load_weight(tok_w1_words, tok_w1_scales, w1_words, w1_plane)
         load_group(1)
+        load_group(2)
         load_weight(tok_w2_words, tok_w2_scales, w2_words, w2_plane)
-        for g in range(2, N_GROUPS):
+        for g in range(3, N_GROUPS):
             load_group(g)
 
         b1_rows = const.tile([P, HIDDEN], BF16)
@@ -105,14 +113,8 @@ def tile_mamba2backbone_pa_t_kernel(
 
         identity = const.tile([P, P], F32)
         make_identity(nc, identity[:])
-        minus_half = const.tile([P, TILES_PER_GROUP], F32)
+        minus_half = const.tile([P, 1], F32)
         nc.gpsimd.memset(minus_half[:], -0.5)
-
-        def clamp_action(g):
-            an = held["u_rows", g][:, :, STOCH:K1]
-            nc.vector.tensor_scalar(out=an, in0=an, scalar1=1.0, scalar2=-1.0, op0=ALU.min, op1=ALU.max)
-
-        clamp_action(0)
 
         b1_sorted = const.tile([P, PACK, P], F32)
         nw_sorted = const.tile([P, PACK, P], F32)
@@ -121,83 +123,98 @@ def tile_mamba2backbone_pa_t_kernel(
         nc.vector.tensor_copy(out=nw_sorted[:], in_=nw_rows[:].rearrange("p (q t) -> p t q", t=PACK))
         nc.vector.tensor_copy(out=b2_f32[:], in_=b2_rows[:])
 
-        def transpose_u(g):
-            u_rows = held["u_rows", g]
-            for pair in range(TILES_PER_GROUP // 2):
+        def is_tile(i):
+            return 0 <= i < N_TILES
+
+        def ends_run(i, length):
+            return is_tile(i) and i % length == length - 1
+
+        def clamp_action(i):
+            if is_tile(i) and i % TILES_PER_GROUP == 0:
+                an = held["u_rows", i // TILES_PER_GROUP][:, :, STOCH:K1]
+                nc.gpsimd.tensor_scalar(out=an, in0=an, scalar1=1.0, scalar2=-1.0, op0=ALU.min, op1=ALU.max)
+
+        def transpose_u(i):
+            if not is_tile(i):
+                return
+            if i % 2 == 0:
                 u_bank = psum_u.tile([P, 2, 2, P], F32)
-                for i in range(2):
-                    words = u_rows[:, 2 * pair + i, :].bitcast(F32)
-                    for half in range(2):
-                        nc.tensor.transpose(u_bank[:, i, half, :], words[:, half : K1 // 2 : 2], identity[:])
-                held["u_bank", g, pair] = u_bank
+                held["u_bank", i // 2] = u_bank
+            words = held["u_rows", i // TILES_PER_GROUP][:, i % TILES_PER_GROUP, :].bitcast(F32)
+            for half in range(2):
+                nc.tensor.transpose(held["u_bank", i // 2][:, i % 2, half, :], words[:, half : K1 // 2 : 2], identity[:])
 
-        def copy_u(g):
-            u_grouped = per_group.tile([P, PACK * GROUP_TOKENS], BF16, align_bytes=64)
-            as_words = u_grouped[:].bitcast(F32).rearrange("p (r i w h) -> p r i w h", r=2, i=2, h=2)
-            for pair in range(TILES_PER_GROUP // 2):
-                nc.scalar.copy(
-                    out=as_words[:, pair],
-                    in_=held["u_bank", g, pair][:].rearrange("p i h w -> p i w h"),
-                )
-            held["u_grouped", g] = u_grouped
+        def copy_u(i):
+            if not ends_run(i, 2):
+                return
+            g = i // TILES_PER_GROUP
+            if i % TILES_PER_GROUP == 1:
+                u_grouped = per_group.tile([P, PACK * GROUP_TOKENS], BF16, align_bytes=64)
+                held["u_grouped", g] = u_grouped
+            as_words = held["u_grouped", g][:].bitcast(F32).rearrange("p (r i w h) -> p r i w h", r=2, i=2, h=2)
+            nc.scalar.copy(
+                out=as_words[:, (i % TILES_PER_GROUP) // 2],
+                in_=held["u_bank", i // 2][:].rearrange("p i h w -> p i w h"),
+            )
 
-        def quantise(name, g):
-            grouped = held[name + "_grouped", g]
+        def quantise(name, i):
+            if not ends_run(i, TILES_PER_GROUP):
+                return
+            g = i // TILES_PER_GROUP
             codes = per_group.tile([P, GROUP_TOKENS], U32, align_bytes=64, tag=name + "_codes")
             scales = per_group.tile([P, GROUP_TOKENS], U8, align_bytes=64, tag=name + "_scales")
-            nc.vector.quantize_mx(out=codes[:].bitcast(FP8X4), scales=scales[:], in_=grouped[:])
+            nc.vector.quantize_mx(out=codes[:].bitcast(FP8X4), scales=scales[:], in_=held[name + "_grouped", g][:])
             held[name + "_codes", g] = codes
             held[name + "_scales", g] = scales
 
-        def first_matmul(g, j):
-            tokens = slice(P * j, P * (j + 1))
+        def first_matmul(i):
+            if not is_tile(i):
+                return
+            g = i // TILES_PER_GROUP
+            tokens = slice(P * (i % TILES_PER_GROUP), P * (i % TILES_PER_GROUP + 1))
             h_bank = psum_h.tile([P, HIDDEN], F32)
-            nc.tensor.matmul_mx(
-                out=h_bank[:],
-                lhsT=held["u_codes", g][:, tokens].bitcast(FP8X4),
-                lhsT_scale=held["u_scales", g][:, tokens],
-                rhs=w1_words[:].bitcast(FP8X4),
-                rhs_scale=w1_plane[:],
-                start=True,
-                stop=True,
-            )
-            held["h_bank", g, j] = h_bank
+            for repeat in range(FIRST_MATMUL_PASSES):
+                nc.tensor.matmul_mx(
+                    out=h_bank[:],
+                    lhsT=held["u_codes", g][:, tokens].bitcast(FP8X4),
+                    lhsT_scale=held["u_scales", g][:, tokens],
+                    rhs=w1_words[:].bitcast(FP8X4),
+                    rhs_scale=w1_plane[:],
+                    start=True,
+                    stop=True,
+                )
+            held["h_bank", i] = h_bank
 
-        def add_bias_and_square(g, j):
-            if j == 0:
-                sum_sq = per_group.tile([P, TILES_PER_GROUP], F32)
-                held["sum_sq", g] = sum_sq
+        def add_bias_and_square(i):
+            if not is_tile(i):
+                return
             h_sorted = per_tile.tile([P, PACK, P], F32)
             nc.vector.tensor_tensor(
                 out=h_sorted[:],
-                in0=held["h_bank", g, j][:].rearrange("p (q t) -> p t q", t=PACK),
+                in0=held["h_bank", i][:].rearrange("p (q t) -> p t q", t=PACK),
                 in1=b1_sorted[:],
                 op=ALU.add,
             )
             squares = per_tile.tile([P, PACK, P], BF16)
-            nc.scalar.activation(
-                out=squares[:], in_=h_sorted[:], func=ACT.Square, accum_out=held["sum_sq", g][:, j : j + 1]
-            )
-            held["h_sorted", g, j] = h_sorted
-
-        def inverse_rms(g):
-            mean_sq = per_group.tile([P, TILES_PER_GROUP], F32)
-            inv_rms = per_group.tile([P, TILES_PER_GROUP], F32)
+            sum_sq = per_tile.tile([P, 1], F32)
+            nc.scalar.activation(out=squares[:], in_=h_sorted[:], func=ACT.Square, accum_out=sum_sq[:])
+            mean_sq = per_tile.tile([P, 1], F32)
+            inv_rms = per_tile.tile([P, 1], F32)
             nc.gpsimd.tensor_scalar(
-                out=mean_sq[:], in0=held["sum_sq", g][:], scalar1=1.0 / HIDDEN, scalar2=EPS, op0=ALU.mult, op1=ALU.add
+                out=mean_sq[:], in0=sum_sq[:], scalar1=1.0 / HIDDEN, scalar2=EPS, op0=ALU.mult, op1=ALU.add
             )
             nc.gpsimd.tensor_tensor(out=inv_rms[:], in0=mean_sq[:], in1=minus_half[:], op=ALU.pow)
-            held["inv_rms", g] = inv_rms
+            held["h_sorted", i] = h_sorted
+            held["inv_rms", i] = inv_rms
 
-        def normalise_transpose_silu(g, j):
-            if j == 0:
-                g_grouped = per_group.tile([P, PACK * GROUP_TOKENS], BF16, align_bytes=64)
-                held["g_grouped", g] = g_grouped
+        def normalise_and_transpose(i):
+            if not is_tile(i):
+                return
             z_sorted = per_tile.tile([P, PACK, P], F32)
             nc.vector.scalar_tensor_tensor(
                 out=z_sorted[:],
-                in0=held["h_sorted", g, j][:],
-                scalar=held["inv_rms", g][:, j : j + 1],
+                in0=held["h_sorted", i][:],
+                scalar=held["inv_rms", i][:],
                 in1=nw_sorted[:],
                 op0=ALU.mult,
                 op1=ALU.mult,
@@ -205,13 +222,26 @@ def tile_mamba2backbone_pa_t_kernel(
             z_bank = psum_z.tile([P, PACK, P], F32)
             for t in range(PACK):
                 nc.tensor.transpose(z_bank[:, t, :], z_sorted[:, t, :], identity[:])
+            held["z_bank", i] = z_bank
+
+        def silu(i):
+            if not is_tile(i):
+                return
+            g = i // TILES_PER_GROUP
+            j = i % TILES_PER_GROUP
+            if j == 0:
+                g_grouped = per_group.tile([P, PACK * GROUP_TOKENS], BF16, align_bytes=64)
+                held["g_grouped", g] = g_grouped
             nc.scalar.activation(
                 out=held["g_grouped", g][:, PACK * P * j : PACK * P * (j + 1)].rearrange("p (w t) -> p w t", t=PACK),
-                in_=z_bank[:].rearrange("p t w -> p w t"),
+                in_=held["z_bank", i][:].rearrange("p t w -> p w t"),
                 func=ACT.Silu,
             )
 
-        def second_matmul(g):
+        def second_matmul(i):
+            if not ends_run(i, TILES_PER_GROUP):
+                return
+            g = i // TILES_PER_GROUP
             o_bank = psum_o.tile([P, TILES_PER_GROUP, DETER], F32)
             for j in range(TILES_PER_GROUP):
                 tokens = slice(P * j, P * (j + 1))
@@ -226,7 +256,10 @@ def tile_mamba2backbone_pa_t_kernel(
                 )
             held["o_bank", g] = o_bank
 
-        def add_bias_and_store(g):
+        def add_bias_and_store(i):
+            if not ends_run(i, TILES_PER_GROUP):
+                return
+            g = i // TILES_PER_GROUP
             o_rows = per_group.tile([P, TILES_PER_GROUP, DETER], F32)
             nc.vector.tensor_tensor(
                 out=o_rows[:],
@@ -236,31 +269,15 @@ def tile_mamba2backbone_pa_t_kernel(
             )
             nc.sync.dma_start(out=out_groups[g], in_=o_rows[:])
 
-        def is_group(g):
-            return 0 <= g < N_GROUPS
-
-        for s in range(-2, N_GROUPS + 2):
-            if is_group(s + 1):
-                copy_u(s + 1)
-            if is_group(s):
-                for j in range(TILES_PER_GROUP):
-                    add_bias_and_square(s, j)
-                    if j + 2 < TILES_PER_GROUP:
-                        first_matmul(s, j + 2)
-                inverse_rms(s)
-            if is_group(s + 3):
-                clamp_action(s + 3)
-            if is_group(s + 2):
-                transpose_u(s + 2)
-            if is_group(s + 1):
-                quantise("u", s + 1)
-                first_matmul(s + 1, 0)
-                first_matmul(s + 1, 1)
-            if is_group(s - 2):
-                quantise("g", s - 2)
-                second_matmul(s - 2)
-            if is_group(s - 1):
-                for j in range(TILES_PER_GROUP):
-                    normalise_transpose_silu(s - 1, j)
-            if is_group(s - 2):
-                add_bias_and_store(s - 2)
+        for i in range(-U_AHEAD - 2, N_TILES + NORM_LAG + 4):
+            clamp_action(i + U_AHEAD + 2)
+            silu(i - NORM_LAG - 1)
+            add_bias_and_square(i)
+            quantise("g", i - NORM_LAG - 2)
+            first_matmul(i + H_AHEAD)
+            second_matmul(i - NORM_LAG - 2)
+            normalise_and_transpose(i - NORM_LAG)
+            transpose_u(i + U_AHEAD)
+            copy_u(i + U_AHEAD - 2)
+            quantise("u", i + U_AHEAD - 4)
+            add_bias_and_store(i - NORM_LAG - 3)

@@ -24,14 +24,8 @@ EPS = 1e-4
 
 TILES_PER_GROUP = 4
 GROUP_TOKENS = P * TILES_PER_GROUP
-N_TILES = TOKENS // P
 N_GROUPS = TOKENS // GROUP_TOKENS
-
-U_AHEAD = 10
-H_AHEAD = 2
-NORM_LAG = 4
-
-FIRST_MATMUL_PASSES = 2
+H_BANKS = 2
 
 FLOPS = 2 * TOKENS * K1 * HIDDEN + 2 * TOKENS * HIDDEN * DETER
 
@@ -59,9 +53,9 @@ def tile_mamba2backbone_pa_t_kernel(
         const = ctx.enter_context(tc.tile_pool(name="const", bufs=1))
         inputs = ctx.enter_context(tc.tile_pool(name="inputs", bufs=N_GROUPS))
         per_group = ctx.enter_context(tc.tile_pool(name="per_group", bufs=3))
-        per_tile = ctx.enter_context(tc.tile_pool(name="per_tile", bufs=NORM_LAG + 2))
+        per_tile = ctx.enter_context(tc.tile_pool(name="per_tile", bufs=2 * TILES_PER_GROUP))
         psum_u = ctx.enter_context(tc.psum_pool(name="psum_u", bufs=2))
-        psum_h = ctx.enter_context(tc.psum_pool(name="psum_h", bufs=H_AHEAD))
+        psum_h = ctx.enter_context(tc.psum_pool(name="psum_h", bufs=H_BANKS))
         psum_z = ctx.enter_context(tc.psum_pool(name="psum_z", bufs=3))
         psum_o = ctx.enter_context(tc.psum_pool(name="psum_o", bufs=1))
         ctx.enter_context(tc.manual_schedule())
@@ -94,18 +88,11 @@ def tile_mamba2backbone_pa_t_kernel(
 
         load_group(0)
         load_weight(tok_w1_words, tok_w1_scales, w1_words, w1_plane)
-        load_group(1)
-        load_group(2)
-        load_weight(tok_w2_words, tok_w2_scales, w2_words, w2_plane)
-        for g in range(3, N_GROUPS):
+        for g in range(1, 4):
             load_group(g)
-
-        b1_rows = const.tile([P, HIDDEN], BF16)
-        nw_rows = const.tile([P, HIDDEN], BF16)
-        b2_rows = const.tile([P, DETER], BF16)
-        nc.scalar.dma_start(out=b1_rows[:], in_=tok_b1.partition_broadcast(P))
-        nc.scalar.dma_start(out=nw_rows[:], in_=tok_nw.partition_broadcast(P))
-        nc.scalar.dma_start(out=b2_rows[:], in_=tok_b2.partition_broadcast(P))
+        load_weight(tok_w2_words, tok_w2_scales, w2_words, w2_plane)
+        for g in range(4, N_GROUPS):
+            load_group(g)
 
         warm = const.tile([P, 1], F32)
         nc.vector.memset(warm[:], 0.0)
@@ -113,108 +100,129 @@ def tile_mamba2backbone_pa_t_kernel(
 
         identity = const.tile([P, P], F32)
         make_identity(nc, identity[:])
-        minus_half = const.tile([P, 1], F32)
+        minus_half = const.tile([P, TILES_PER_GROUP], F32)
         nc.gpsimd.memset(minus_half[:], -0.5)
 
+        ones = const.tile([P, P], BF16)
+        nc.vector.memset(ones[:], 1.0)
+        vector_rows = const.tile([P, 2 * HIDDEN + DETER], BF16)
+        nc.vector.memset(vector_rows[:], 0.0)
+        nc.scalar.dma_start(out=vector_rows[0:1, 0:HIDDEN], in_=tok_b1.unsqueeze(0))
+        nc.scalar.dma_start(out=vector_rows[0:1, HIDDEN : 2 * HIDDEN], in_=tok_nw.unsqueeze(0))
+        nc.scalar.dma_start(out=vector_rows[0:1, 2 * HIDDEN : 2 * HIDDEN + DETER], in_=tok_b2.unsqueeze(0))
         b1_sorted = const.tile([P, PACK, P], F32)
         nw_sorted = const.tile([P, PACK, P], F32)
-        b2_f32 = const.tile([P, DETER], F32)
-        nc.vector.tensor_copy(out=b1_sorted[:], in_=b1_rows[:].rearrange("p (q t) -> p t q", t=PACK))
-        nc.vector.tensor_copy(out=nw_sorted[:], in_=nw_rows[:].rearrange("p (q t) -> p t q", t=PACK))
-        nc.vector.tensor_copy(out=b2_f32[:], in_=b2_rows[:])
+        b2_spread = const.tile([P, DETER], F32)
 
-        def is_tile(i):
-            return 0 <= i < N_TILES
-
-        def ends_run(i, length):
-            return is_tile(i) and i % length == length - 1
-
-        def clamp_action(i):
-            if is_tile(i) and i % TILES_PER_GROUP == 0:
-                an = held["u_rows", i // TILES_PER_GROUP][:, :, STOCH:K1]
-                nc.gpsimd.tensor_scalar(out=an, in0=an, scalar1=1.0, scalar2=-1.0, op0=ALU.min, op1=ALU.max)
-
-        def transpose_u(i):
-            if not is_tile(i):
-                return
-            if i % 2 == 0:
-                u_bank = psum_u.tile([P, 2, 2, P], F32)
-                held["u_bank", i // 2] = u_bank
-            words = held["u_rows", i // TILES_PER_GROUP][:, i % TILES_PER_GROUP, :].bitcast(F32)
-            for half in range(2):
-                nc.tensor.transpose(held["u_bank", i // 2][:, i % 2, half, :], words[:, half : K1 // 2 : 2], identity[:])
-
-        def copy_u(i):
-            if not ends_run(i, 2):
-                return
-            g = i // TILES_PER_GROUP
-            if i % TILES_PER_GROUP == 1:
-                u_grouped = per_group.tile([P, PACK * GROUP_TOKENS], BF16, align_bytes=64)
-                held["u_grouped", g] = u_grouped
-            as_words = held["u_grouped", g][:].bitcast(F32).rearrange("p (r i w h) -> p r i w h", r=2, i=2, h=2)
-            nc.scalar.copy(
-                out=as_words[:, (i % TILES_PER_GROUP) // 2],
-                in_=held["u_bank", i // 2][:].rearrange("p i h w -> p i w h"),
+        def spread(first, width):
+            h_bank = psum_h.tile([P, HIDDEN], F32)
+            nc.tensor.matmul(
+                out=h_bank[:, 0:width], lhsT=ones[:], rhs=vector_rows[:, first : first + width], start=True, stop=True
             )
+            return h_bank
 
-        def quantise(name, i):
-            if not ends_run(i, TILES_PER_GROUP):
+        nc.scalar.copy(out=b1_sorted[:], in_=spread(0, HIDDEN)[:].rearrange("p (q t) -> p t q", t=PACK))
+        nc.scalar.copy(out=nw_sorted[:], in_=spread(HIDDEN, HIDDEN)[:].rearrange("p (q t) -> p t q", t=PACK))
+        nc.scalar.copy(out=b2_spread[:], in_=spread(2 * HIDDEN, DETER)[:, 0:DETER])
+
+        def is_group(g):
+            return 0 <= g < N_GROUPS
+
+        def clamp_action(g):
+            if is_group(g):
+                an = held["u_rows", g][:, :, STOCH:K1]
+                nc.vector.tensor_scalar(out=an, in0=an, scalar1=1.0, scalar2=-1.0, op0=ALU.min, op1=ALU.max)
+
+        def transpose_u(g, j):
+            if not is_group(g):
                 return
-            g = i // TILES_PER_GROUP
+            if j % 2 == 0:
+                u_bank = psum_u.tile([P, 2, 2, P], F32)
+                held["u_bank", g, j // 2] = u_bank
+            words = held["u_rows", g][:, j, :].bitcast(F32)
+            for half in range(2):
+                nc.tensor.transpose(
+                    held["u_bank", g, j // 2][:, j % 2, half, :], words[:, half : K1 // 2 : 2], identity[:]
+                )
+
+        def copy_u(g):
+            if not is_group(g):
+                return
+            u_grouped = per_group.tile([P, PACK * GROUP_TOKENS], BF16, align_bytes=64)
+            as_words = u_grouped[:].bitcast(F32).rearrange("p (r i w h) -> p r i w h", r=2, i=2, h=2)
+            for pair in range(TILES_PER_GROUP // 2):
+                nc.scalar.copy(
+                    out=as_words[:, pair],
+                    in_=held["u_bank", g, pair][:].rearrange("p i h w -> p i w h"),
+                )
+            held["u_grouped", g] = u_grouped
+
+        def quantise(name, g):
+            if not is_group(g):
+                return
             codes = per_group.tile([P, GROUP_TOKENS], U32, align_bytes=64, tag=name + "_codes")
             scales = per_group.tile([P, GROUP_TOKENS], U8, align_bytes=64, tag=name + "_scales")
             nc.vector.quantize_mx(out=codes[:].bitcast(FP8X4), scales=scales[:], in_=held[name + "_grouped", g][:])
             held[name + "_codes", g] = codes
             held[name + "_scales", g] = scales
 
-        def first_matmul(i):
-            if not is_tile(i):
+        def first_matmul(g, j):
+            if not is_group(g):
                 return
-            g = i // TILES_PER_GROUP
-            tokens = slice(P * (i % TILES_PER_GROUP), P * (i % TILES_PER_GROUP + 1))
+            tokens = slice(P * j, P * (j + 1))
             h_bank = psum_h.tile([P, HIDDEN], F32)
-            for repeat in range(FIRST_MATMUL_PASSES):
-                nc.tensor.matmul_mx(
-                    out=h_bank[:],
-                    lhsT=held["u_codes", g][:, tokens].bitcast(FP8X4),
-                    lhsT_scale=held["u_scales", g][:, tokens],
-                    rhs=w1_words[:].bitcast(FP8X4),
-                    rhs_scale=w1_plane[:],
-                    start=True,
-                    stop=True,
-                )
-            held["h_bank", i] = h_bank
+            nc.tensor.matmul_mx(
+                out=h_bank[:],
+                lhsT=held["u_codes", g][:, tokens].bitcast(FP8X4),
+                lhsT_scale=held["u_scales", g][:, tokens],
+                rhs=w1_words[:].bitcast(FP8X4),
+                rhs_scale=w1_plane[:],
+                start=True,
+                stop=True,
+            )
+            held["h_bank", g, j] = h_bank
 
-        def add_bias_and_square(i):
-            if not is_tile(i):
+        def add_bias_and_square(g, j):
+            if not is_group(g):
                 return
+            if j == 0:
+                sum_sq = per_group.tile([P, TILES_PER_GROUP], F32)
+                held["sum_sq", g] = sum_sq
             h_sorted = per_tile.tile([P, PACK, P], F32)
             nc.vector.tensor_tensor(
                 out=h_sorted[:],
-                in0=held["h_bank", i][:].rearrange("p (q t) -> p t q", t=PACK),
+                in0=held["h_bank", g, j][:].rearrange("p (q t) -> p t q", t=PACK),
                 in1=b1_sorted[:],
                 op=ALU.add,
             )
             squares = per_tile.tile([P, PACK, P], BF16)
-            sum_sq = per_tile.tile([P, 1], F32)
-            nc.scalar.activation(out=squares[:], in_=h_sorted[:], func=ACT.Square, accum_out=sum_sq[:])
-            mean_sq = per_tile.tile([P, 1], F32)
-            inv_rms = per_tile.tile([P, 1], F32)
+            nc.scalar.activation(
+                out=squares[:], in_=h_sorted[:], func=ACT.Square, accum_out=held["sum_sq", g][:, j : j + 1]
+            )
+            held["h_sorted", g, j] = h_sorted
+
+        def inverse_rms(g):
+            if not is_group(g):
+                return
+            mean_sq = per_group.tile([P, TILES_PER_GROUP], F32)
+            inv_rms = per_group.tile([P, TILES_PER_GROUP], F32)
             nc.gpsimd.tensor_scalar(
-                out=mean_sq[:], in0=sum_sq[:], scalar1=1.0 / HIDDEN, scalar2=EPS, op0=ALU.mult, op1=ALU.add
+                out=mean_sq[:], in0=held["sum_sq", g][:], scalar1=1.0 / HIDDEN, scalar2=EPS, op0=ALU.mult, op1=ALU.add
             )
             nc.gpsimd.tensor_tensor(out=inv_rms[:], in0=mean_sq[:], in1=minus_half[:], op=ALU.pow)
-            held["h_sorted", i] = h_sorted
-            held["inv_rms", i] = inv_rms
+            held["inv_rms", g] = inv_rms
 
-        def normalise_and_transpose(i):
-            if not is_tile(i):
+        def normalise_transpose_silu(g, j):
+            if not is_group(g):
                 return
+            if j == 0:
+                g_grouped = per_group.tile([P, PACK * GROUP_TOKENS], BF16, align_bytes=64)
+                held["g_grouped", g] = g_grouped
             z_sorted = per_tile.tile([P, PACK, P], F32)
             nc.vector.scalar_tensor_tensor(
                 out=z_sorted[:],
-                in0=held["h_sorted", i][:],
-                scalar=held["inv_rms", i][:],
+                in0=held["h_sorted", g, j][:],
+                scalar=held["inv_rms", g][:, j : j + 1],
                 in1=nw_sorted[:],
                 op0=ALU.mult,
                 op1=ALU.mult,
@@ -222,26 +230,15 @@ def tile_mamba2backbone_pa_t_kernel(
             z_bank = psum_z.tile([P, PACK, P], F32)
             for t in range(PACK):
                 nc.tensor.transpose(z_bank[:, t, :], z_sorted[:, t, :], identity[:])
-            held["z_bank", i] = z_bank
-
-        def silu(i):
-            if not is_tile(i):
-                return
-            g = i // TILES_PER_GROUP
-            j = i % TILES_PER_GROUP
-            if j == 0:
-                g_grouped = per_group.tile([P, PACK * GROUP_TOKENS], BF16, align_bytes=64)
-                held["g_grouped", g] = g_grouped
             nc.scalar.activation(
                 out=held["g_grouped", g][:, PACK * P * j : PACK * P * (j + 1)].rearrange("p (w t) -> p w t", t=PACK),
-                in_=held["z_bank", i][:].rearrange("p t w -> p w t"),
+                in_=z_bank[:].rearrange("p t w -> p w t"),
                 func=ACT.Silu,
             )
 
-        def second_matmul(i):
-            if not ends_run(i, TILES_PER_GROUP):
+        def second_matmul(g):
+            if not is_group(g):
                 return
-            g = i // TILES_PER_GROUP
             o_bank = psum_o.tile([P, TILES_PER_GROUP, DETER], F32)
             for j in range(TILES_PER_GROUP):
                 tokens = slice(P * j, P * (j + 1))
@@ -256,28 +253,31 @@ def tile_mamba2backbone_pa_t_kernel(
                 )
             held["o_bank", g] = o_bank
 
-        def add_bias_and_store(i):
-            if not ends_run(i, TILES_PER_GROUP):
+        def add_bias_and_store(g):
+            if not is_group(g):
                 return
-            g = i // TILES_PER_GROUP
             o_rows = per_group.tile([P, TILES_PER_GROUP, DETER], F32)
             nc.vector.tensor_tensor(
                 out=o_rows[:],
                 in0=held["o_bank", g][:],
-                in1=b2_f32[:].unsqueeze(1).to_broadcast([P, TILES_PER_GROUP, DETER]),
+                in1=b2_spread[:].unsqueeze(1).to_broadcast([P, TILES_PER_GROUP, DETER]),
                 op=ALU.add,
             )
             nc.sync.dma_start(out=out_groups[g], in_=o_rows[:])
 
-        for i in range(-U_AHEAD - 2, N_TILES + NORM_LAG + 4):
-            clamp_action(i + U_AHEAD + 2)
-            silu(i - NORM_LAG - 1)
-            add_bias_and_square(i)
-            quantise("g", i - NORM_LAG - 2)
-            first_matmul(i + H_AHEAD)
-            second_matmul(i - NORM_LAG - 2)
-            normalise_and_transpose(i - NORM_LAG)
-            transpose_u(i + U_AHEAD)
-            copy_u(i + U_AHEAD - 2)
-            quantise("u", i + U_AHEAD - 4)
-            add_bias_and_store(i - NORM_LAG - 3)
+        for s in range(-3, N_GROUPS + 3):
+            for j in range(TILES_PER_GROUP):
+                add_bias_and_square(s, j)
+                ahead = TILES_PER_GROUP * s + j + H_BANKS
+                first_matmul(ahead // TILES_PER_GROUP, ahead % TILES_PER_GROUP)
+                if j == H_BANKS - 1:
+                    quantise("u", s + 1)
+                    second_matmul(s - 3)
+            inverse_rms(s)
+            clamp_action(s + 3)
+            copy_u(s + 2)
+            for j in range(TILES_PER_GROUP):
+                normalise_transpose_silu(s - 1, j)
+                transpose_u(s + 3, j)
+            add_bias_and_store(s - 3)
+            quantise("g", s - 2)

@@ -22,9 +22,11 @@ HIDDEN = 512
 DETER = 128
 EPS = 1e-4
 
-TILES_PER_GROUP = 4
-GROUP_TOKENS = P * TILES_PER_GROUP
-N_GROUPS = TOKENS // GROUP_TOKENS
+MAX_TILES = 4
+GROUP_TILES = [2, 2, 2] + [MAX_TILES] * 14 + [2]
+N_GROUPS = len(GROUP_TILES)
+FIRST_TILE = [sum(GROUP_TILES[:g]) for g in range(N_GROUPS)]
+TILE_LIST = [(g, j) for g in range(N_GROUPS) for j in range(GROUP_TILES[g])]
 H_BANKS = 2
 
 FLOPS = 2 * TOKENS * K1 * HIDDEN + 2 * TOKENS * HIDDEN * DETER
@@ -45,15 +47,15 @@ def tile_mamba2backbone_pa_t_kernel(
 ):
     nc = tc.nc
 
-    stoch_groups = stoch.rearrange("(g p j) k -> g p j k", p=P, j=TILES_PER_GROUP)
-    action_groups = action.rearrange("(g p j) k -> g p j k", p=P, j=TILES_PER_GROUP)
-    out_groups = out.rearrange("(g p j) n -> g p j n", p=P, j=TILES_PER_GROUP)
+    def group_rows(tensor, g):
+        first = P * FIRST_TILE[g]
+        return tensor[first : first + P * GROUP_TILES[g], :].rearrange("(p j) k -> p j k", j=GROUP_TILES[g])
 
     with ExitStack() as ctx:
         const = ctx.enter_context(tc.tile_pool(name="const", bufs=1))
         inputs = ctx.enter_context(tc.tile_pool(name="inputs", bufs=N_GROUPS))
         per_group = ctx.enter_context(tc.tile_pool(name="per_group", bufs=3))
-        per_tile = ctx.enter_context(tc.tile_pool(name="per_tile", bufs=2 * TILES_PER_GROUP))
+        per_tile = ctx.enter_context(tc.tile_pool(name="per_tile", bufs=2 * MAX_TILES))
         psum_u = ctx.enter_context(tc.psum_pool(name="psum_u", bufs=2))
         psum_h = ctx.enter_context(tc.psum_pool(name="psum_h", bufs=H_BANKS))
         psum_z = ctx.enter_context(tc.psum_pool(name="psum_z", bufs=3))
@@ -63,9 +65,9 @@ def tile_mamba2backbone_pa_t_kernel(
         held = {}
 
         def load_group(g):
-            u_rows = inputs.tile([P, TILES_PER_GROUP, K1], BF16)
-            nc.sync.dma_start(out=u_rows[:, :, STOCH:K1], in_=action_groups[g])
-            nc.sync.dma_start(out=u_rows[:, :, 0:STOCH], in_=stoch_groups[g])
+            u_rows = inputs.tile([P, GROUP_TILES[g], K1], BF16)
+            nc.sync.dma_start(out=u_rows[:, :, STOCH:K1], in_=group_rows(action, g))
+            nc.sync.dma_start(out=u_rows[:, :, 0:STOCH], in_=group_rows(stoch, g))
             held["u_rows", g] = u_rows
 
         def load_weight(words_dram, scales_dram, words, plane):
@@ -84,12 +86,27 @@ def tile_mamba2backbone_pa_t_kernel(
         w2_words = const.tile([P, PACK * DETER], U8, align_bytes=64)
         w2_plane = const.tile([P, DETER], U8, align_bytes=64)
         nc.vector.memset(w1_plane[:].bitcast(I32), 0)
-        nc.vector.memset(w2_plane[:].bitcast(I32), 0)
+
+        def row_of_zeros(width, name):
+            rows = const.tile([P, width], BF16, name=name)
+            nc.vector.memset(rows[:], 0.0)
+            return rows
+
+        b1_row = row_of_zeros(HIDDEN, "b1_row")
+        nw_row = row_of_zeros(HIDDEN, "nw_row")
+        b2_row = row_of_zeros(DETER, "b2_row")
+        ones = const.tile([P, P], BF16)
+        nc.vector.memset(ones[:], 1.0)
 
         load_group(0)
         load_weight(tok_w1_words, tok_w1_scales, w1_words, w1_plane)
-        for g in range(1, 4):
-            load_group(g)
+        nc.sync.dma_start(out=b1_row[0:1, :], in_=tok_b1.unsqueeze(0))
+        load_group(1)
+        nc.sync.dma_start(out=nw_row[0:1, :], in_=tok_nw.unsqueeze(0))
+        nc.sync.dma_start(out=b2_row[0:1, :], in_=tok_b2.unsqueeze(0))
+        load_group(2)
+        load_group(3)
+        nc.vector.memset(w2_plane[:].bitcast(I32), 0)
         load_weight(tok_w2_words, tok_w2_scales, w2_words, w2_plane)
         for g in range(4, N_GROUPS):
             load_group(g)
@@ -100,33 +117,33 @@ def tile_mamba2backbone_pa_t_kernel(
 
         identity = const.tile([P, P], F32)
         make_identity(nc, identity[:])
-        minus_half = const.tile([P, TILES_PER_GROUP], F32)
+        minus_half = const.tile([P, MAX_TILES], F32)
         nc.gpsimd.memset(minus_half[:], -0.5)
 
-        ones = const.tile([P, P], BF16)
-        nc.vector.memset(ones[:], 1.0)
-        vector_rows = const.tile([P, 2 * HIDDEN + DETER], BF16)
-        nc.vector.memset(vector_rows[:], 0.0)
-        nc.scalar.dma_start(out=vector_rows[0:1, 0:HIDDEN], in_=tok_b1.unsqueeze(0))
-        nc.scalar.dma_start(out=vector_rows[0:1, HIDDEN : 2 * HIDDEN], in_=tok_nw.unsqueeze(0))
-        nc.scalar.dma_start(out=vector_rows[0:1, 2 * HIDDEN : 2 * HIDDEN + DETER], in_=tok_b2.unsqueeze(0))
         b1_sorted = const.tile([P, PACK, P], F32)
         nw_sorted = const.tile([P, PACK, P], F32)
         b2_spread = const.tile([P, DETER], F32)
 
-        def spread(first, width):
-            h_bank = psum_h.tile([P, HIDDEN], F32)
-            nc.tensor.matmul(
-                out=h_bank[:, 0:width], lhsT=ones[:], rhs=vector_rows[:, first : first + width], start=True, stop=True
-            )
-            return h_bank
+        def spread(row, width):
+            z_bank = psum_z.tile([P, HIDDEN], F32)
+            nc.tensor.matmul(out=z_bank[:, 0:width], lhsT=ones[:], rhs=row[:], start=True, stop=True)
+            return z_bank
 
-        nc.scalar.copy(out=b1_sorted[:], in_=spread(0, HIDDEN)[:].rearrange("p (q t) -> p t q", t=PACK))
-        nc.scalar.copy(out=nw_sorted[:], in_=spread(HIDDEN, HIDDEN)[:].rearrange("p (q t) -> p t q", t=PACK))
-        nc.scalar.copy(out=b2_spread[:], in_=spread(2 * HIDDEN, DETER)[:, 0:DETER])
+        def spread_b1():
+            b1_bank = spread(b1_row, HIDDEN)
+            nc.vector.tensor_copy(out=b1_sorted[:], in_=b1_bank[:].rearrange("p (q t) -> p t q", t=PACK))
+
+        def spread_norm_and_b2():
+            nw_bank = spread(nw_row, HIDDEN)
+            b2_bank = spread(b2_row, DETER)
+            nc.scalar.copy(out=nw_sorted[:], in_=nw_bank[:].rearrange("p (q t) -> p t q", t=PACK))
+            nc.scalar.copy(out=b2_spread[:], in_=b2_bank[:, 0:DETER])
 
         def is_group(g):
             return 0 <= g < N_GROUPS
+
+        def is_tile(g, j):
+            return is_group(g) and j < GROUP_TILES[g]
 
         def clamp_action(g):
             if is_group(g):
@@ -134,7 +151,7 @@ def tile_mamba2backbone_pa_t_kernel(
                 nc.vector.tensor_scalar(out=an, in0=an, scalar1=1.0, scalar2=-1.0, op0=ALU.min, op1=ALU.max)
 
         def transpose_u(g, j):
-            if not is_group(g):
+            if not is_tile(g, j):
                 return
             if j % 2 == 0:
                 u_bank = psum_u.tile([P, 2, 2, P], F32)
@@ -148,9 +165,10 @@ def tile_mamba2backbone_pa_t_kernel(
         def copy_u(g):
             if not is_group(g):
                 return
-            u_grouped = per_group.tile([P, PACK * GROUP_TOKENS], BF16, align_bytes=64)
-            as_words = u_grouped[:].bitcast(F32).rearrange("p (r i w h) -> p r i w h", r=2, i=2, h=2)
-            for pair in range(TILES_PER_GROUP // 2):
+            pairs = GROUP_TILES[g] // 2
+            u_grouped = per_group.tile([P, PACK * P * GROUP_TILES[g]], BF16, align_bytes=64)
+            as_words = u_grouped[:].bitcast(F32).rearrange("p (r i w h) -> p r i w h", r=pairs, i=2, h=2)
+            for pair in range(pairs):
                 nc.scalar.copy(
                     out=as_words[:, pair],
                     in_=held["u_bank", g, pair][:].rearrange("p i h w -> p i w h"),
@@ -160,15 +178,13 @@ def tile_mamba2backbone_pa_t_kernel(
         def quantise(name, g):
             if not is_group(g):
                 return
-            codes = per_group.tile([P, GROUP_TOKENS], U32, align_bytes=64, tag=name + "_codes")
-            scales = per_group.tile([P, GROUP_TOKENS], U8, align_bytes=64, tag=name + "_scales")
+            codes = per_group.tile([P, P * GROUP_TILES[g]], U32, align_bytes=64, tag=name + "_codes")
+            scales = per_group.tile([P, P * GROUP_TILES[g]], U8, align_bytes=64, tag=name + "_scales")
             nc.vector.quantize_mx(out=codes[:].bitcast(FP8X4), scales=scales[:], in_=held[name + "_grouped", g][:])
             held[name + "_codes", g] = codes
             held[name + "_scales", g] = scales
 
         def first_matmul(g, j):
-            if not is_group(g):
-                return
             tokens = slice(P * j, P * (j + 1))
             h_bank = psum_h.tile([P, HIDDEN], F32)
             nc.tensor.matmul_mx(
@@ -182,11 +198,19 @@ def tile_mamba2backbone_pa_t_kernel(
             )
             held["h_bank", g, j] = h_bank
 
+        multiplied = []
+
+        def first_matmuls(emptied):
+            while len(multiplied) < min(emptied + H_BANKS, len(TILE_LIST)):
+                g, j = TILE_LIST[len(multiplied)]
+                if ("u_codes", g) not in held:
+                    return
+                first_matmul(g, j)
+                multiplied.append((g, j))
+
         def add_bias_and_square(g, j):
-            if not is_group(g):
-                return
             if j == 0:
-                sum_sq = per_group.tile([P, TILES_PER_GROUP], F32)
+                sum_sq = per_group.tile([P, GROUP_TILES[g]], F32)
                 held["sum_sq", g] = sum_sq
             h_sorted = per_tile.tile([P, PACK, P], F32)
             nc.vector.tensor_tensor(
@@ -204,19 +228,19 @@ def tile_mamba2backbone_pa_t_kernel(
         def inverse_rms(g):
             if not is_group(g):
                 return
-            mean_sq = per_group.tile([P, TILES_PER_GROUP], F32)
-            inv_rms = per_group.tile([P, TILES_PER_GROUP], F32)
+            mean_sq = per_group.tile([P, GROUP_TILES[g]], F32)
+            inv_rms = per_group.tile([P, GROUP_TILES[g]], F32)
             nc.gpsimd.tensor_scalar(
                 out=mean_sq[:], in0=held["sum_sq", g][:], scalar1=1.0 / HIDDEN, scalar2=EPS, op0=ALU.mult, op1=ALU.add
             )
-            nc.gpsimd.tensor_tensor(out=inv_rms[:], in0=mean_sq[:], in1=minus_half[:], op=ALU.pow)
+            nc.gpsimd.tensor_tensor(out=inv_rms[:], in0=mean_sq[:], in1=minus_half[:, 0 : GROUP_TILES[g]], op=ALU.pow)
             held["inv_rms", g] = inv_rms
 
         def normalise_transpose_silu(g, j):
-            if not is_group(g):
+            if not is_tile(g, j):
                 return
             if j == 0:
-                g_grouped = per_group.tile([P, PACK * GROUP_TOKENS], BF16, align_bytes=64)
+                g_grouped = per_group.tile([P, PACK * P * GROUP_TILES[g]], BF16, align_bytes=64)
                 held["g_grouped", g] = g_grouped
             z_sorted = per_tile.tile([P, PACK, P], F32)
             nc.vector.scalar_tensor_tensor(
@@ -239,8 +263,8 @@ def tile_mamba2backbone_pa_t_kernel(
         def second_matmul(g):
             if not is_group(g):
                 return
-            o_bank = psum_o.tile([P, TILES_PER_GROUP, DETER], F32)
-            for j in range(TILES_PER_GROUP):
+            o_bank = psum_o.tile([P, GROUP_TILES[g], DETER], F32)
+            for j in range(GROUP_TILES[g]):
                 tokens = slice(P * j, P * (j + 1))
                 nc.tensor.matmul_mx(
                     out=o_bank[:, j, :],
@@ -256,28 +280,44 @@ def tile_mamba2backbone_pa_t_kernel(
         def add_bias_and_store(g):
             if not is_group(g):
                 return
-            o_rows = per_group.tile([P, TILES_PER_GROUP, DETER], F32)
+            o_rows = per_group.tile([P, GROUP_TILES[g], DETER], F32)
             nc.vector.tensor_tensor(
                 out=o_rows[:],
                 in0=held["o_bank", g][:],
-                in1=b2_spread[:].unsqueeze(1).to_broadcast([P, TILES_PER_GROUP, DETER]),
+                in1=b2_spread[:].unsqueeze(1).to_broadcast([P, GROUP_TILES[g], DETER]),
                 op=ALU.add,
             )
-            nc.sync.dma_start(out=out_groups[g], in_=o_rows[:])
+            nc.sync.dma_start(out=group_rows(out, g), in_=o_rows[:])
 
         for s in range(-3, N_GROUPS + 3):
-            for j in range(TILES_PER_GROUP):
+            if s == -2:
+                spread_b1()
+            tiles = GROUP_TILES[s] if is_group(s) else 0
+            for j in range(tiles):
                 add_bias_and_square(s, j)
-                ahead = TILES_PER_GROUP * s + j + H_BANKS
-                first_matmul(ahead // TILES_PER_GROUP, ahead % TILES_PER_GROUP)
+                first_matmuls(FIRST_TILE[s] + j + 1)
                 if j == H_BANKS - 1:
                     quantise("u", s + 1)
+                    first_matmuls(FIRST_TILE[s] + j + 1)
                     second_matmul(s - 3)
+            if tiles == 0:
+                quantise("u", s + 1)
+                first_matmuls(0)
+                second_matmul(s - 3)
             inverse_rms(s)
-            clamp_action(s + 3)
+            entering = [0] if s == -3 else [] if s == -2 else [1] if s == -1 else [2, 3] if s == 0 else [s + 3]
+            for g in entering:
+                clamp_action(g)
+            if s == -1 or s == 0:
+                for j in range(GROUP_TILES[s + 2]):
+                    transpose_u(s + 2, j)
+                entering = entering[1:]
             copy_u(s + 2)
-            for j in range(TILES_PER_GROUP):
+            if s == -1:
+                spread_norm_and_b2()
+            for j in range(MAX_TILES):
                 normalise_transpose_silu(s - 1, j)
-                transpose_u(s + 3, j)
+                for g in entering:
+                    transpose_u(g, j)
             add_bias_and_store(s - 3)
             quantise("g", s - 2)

@@ -292,32 +292,29 @@ def tile_mamba2backbone_pa_t_kernel(
         for s in range(-3, N_GROUPS + 3):
             if s == -2:
                 spread_b1()
+            if s >= 1:
+                copy_u(s + 2)
             tiles = GROUP_TILES[s] if is_group(s) else 0
-            for j in range(tiles):
-                add_bias_and_square(s, j)
-                first_matmuls(FIRST_TILE[s] + j + 1)
+            for j in range(max(tiles, H_BANKS)):
+                if j < tiles:
+                    add_bias_and_square(s, j)
+                    first_matmuls(FIRST_TILE[s] + j + 1)
                 if j == H_BANKS - 1:
                     quantise("u", s + 1)
-                    first_matmuls(FIRST_TILE[s] + j + 1)
+                    first_matmuls(FIRST_TILE[s] + j + 1 if tiles else 0)
                     second_matmul(s - 3)
-            if tiles == 0:
-                quantise("u", s + 1)
-                first_matmuls(0)
-                second_matmul(s - 3)
+                    for g in [0] if s == -3 else [] if s == -2 else [1] if s == -1 else [2, 3] if s == 0 else [s + 3]:
+                        clamp_action(g)
+                        for k in range(MAX_TILES):
+                            transpose_u(g, k)
+                        if g == s + 2:
+                            copy_u(g)
             inverse_rms(s)
-            entering = [0] if s == -3 else [] if s == -2 else [1] if s == -1 else [2, 3] if s == 0 else [s + 3]
-            for g in entering:
-                clamp_action(g)
-            if s == -1 or s == 0:
-                for j in range(GROUP_TILES[s + 2]):
-                    transpose_u(s + 2, j)
-                entering = entering[1:]
-            copy_u(s + 2)
+            if s == -2:
+                copy_u(0)
             if s == -1:
                 spread_norm_and_b2()
             for j in range(MAX_TILES):
                 normalise_transpose_silu(s - 1, j)
-                for g in entering:
-                    transpose_u(g, j)
             add_bias_and_store(s - 3)
             quantise("g", s - 2)

@@ -27,6 +27,7 @@ GROUP_TILES = [2, 2, 2] + [MAX_TILES] * 14 + [2]
 N_GROUPS = len(GROUP_TILES)
 FIRST_TILE = [sum(GROUP_TILES[:g]) for g in range(N_GROUPS)]
 TILE_LIST = [(g, j) for g in range(N_GROUPS) for j in range(GROUP_TILES[g])]
+TIMES = 2
 H_BANKS = 2
 
 FLOPS = 2 * TOKENS * K1 * HIDDEN + 2 * TOKENS * HIDDEN * DETER
@@ -162,6 +163,11 @@ def tile_mamba2backbone_pa_t_kernel(
                     held["u_bank", g, j // 2][:, j % 2, half, :], words[:, half : K1 // 2 : 2], identity[:]
                 )
 
+        def enter(g):
+            clamp_action(g)
+            for j in range(MAX_TILES):
+                transpose_u(g, j)
+
         def copy_u(g):
             if not is_group(g):
                 return
@@ -184,18 +190,21 @@ def tile_mamba2backbone_pa_t_kernel(
             held[name + "_codes", g] = codes
             held[name + "_scales", g] = scales
 
-        def first_matmul(g, j):
+        def first_matmul(g, j, times=1):
+            if not is_tile(g, j):
+                return
             tokens = slice(P * j, P * (j + 1))
             h_bank = psum_h.tile([P, HIDDEN], F32)
-            nc.tensor.matmul_mx(
-                out=h_bank[:],
-                lhsT=held["u_codes", g][:, tokens].bitcast(FP8X4),
-                lhsT_scale=held["u_scales", g][:, tokens],
-                rhs=w1_words[:].bitcast(FP8X4),
-                rhs_scale=w1_plane[:],
-                start=True,
-                stop=True,
-            )
+            for repeat in range(times):
+                nc.tensor.matmul_mx(
+                    out=h_bank[:],
+                    lhsT=held["u_codes", g][:, tokens].bitcast(FP8X4),
+                    lhsT_scale=held["u_scales", g][:, tokens],
+                    rhs=w1_words[:].bitcast(FP8X4),
+                    rhs_scale=w1_plane[:],
+                    start=True,
+                    stop=True,
+                )
             held["h_bank", g, j] = h_bank
 
         multiplied = []
@@ -263,7 +272,10 @@ def tile_mamba2backbone_pa_t_kernel(
         def second_matmul(g):
             if not is_group(g):
                 return
-            o_bank = psum_o.tile([P, GROUP_TILES[g], DETER], F32)
+            if g == N_GROUPS - 1:
+                o_bank = psum_h.tile([P, GROUP_TILES[g], DETER], F32, name="o_bank_last", tag="h_bank")
+            else:
+                o_bank = psum_o.tile([P, GROUP_TILES[g], DETER], F32, name="o_bank")
             for j in range(GROUP_TILES[g]):
                 tokens = slice(P * j, P * (j + 1))
                 nc.tensor.matmul_mx(
@@ -290,31 +302,43 @@ def tile_mamba2backbone_pa_t_kernel(
             nc.sync.dma_start(out=group_rows(out, g), in_=o_rows[:])
 
         for s in range(-3, N_GROUPS + 3):
-            if s == -2:
-                spread_b1()
-            if s >= 1:
+            if s != 0 and s >= -1:
                 copy_u(s + 2)
             tiles = GROUP_TILES[s] if is_group(s) else 0
             for j in range(max(tiles, H_BANKS)):
                 if j < tiles:
                     add_bias_and_square(s, j)
-                    first_matmuls(FIRST_TILE[s] + j + 1)
+                    if s < 2:
+                        first_matmuls(FIRST_TILE[s] + j + 1)
+                    elif j + H_BANKS < tiles:
+                        first_matmul(s, j + H_BANKS)
+                if s == 0 and j == 0:
+                    enter(2)
+                    copy_u(2)
                 if j == H_BANKS - 1:
-                    quantise("u", s + 1)
-                    first_matmuls(FIRST_TILE[s] + j + 1 if tiles else 0)
+                    if s != 0:
+                        quantise("u", s + 1)
+                    if s == -1:
+                        spread_b1()
+                    if s < 2:
+                        first_matmuls(FIRST_TILE[s] + j + 1 if tiles else 0)
+                    if s == -1:
+                        quantise("u", 1)
                     second_matmul(s - 3)
-                    for g in [0] if s == -3 else [] if s == -2 else [1] if s == -1 else [2, 3] if s == 0 else [s + 3]:
-                        clamp_action(g)
-                        for k in range(MAX_TILES):
-                            transpose_u(g, k)
-                        if g == s + 2:
-                            copy_u(g)
+                    if s < -1 or s >= 0:
+                        enter(s + 3)
             inverse_rms(s)
             if s == -2:
                 copy_u(0)
             if s == -1:
                 spread_norm_and_b2()
             for j in range(MAX_TILES):
+                if j % 2 == 0 and s >= 2:
+                    first_matmul(s + 1, j // 2, times=TIMES)
                 normalise_transpose_silu(s - 1, j)
-            add_bias_and_store(s - 3)
-            quantise("g", s - 2)
+            if s < N_GROUPS:
+                add_bias_and_store(s - 3)
+                quantise("g", s - 2)
+            else:
+                quantise("g", s - 2)
+                add_bias_and_store(s - 3)

@@ -56,6 +56,7 @@ def tile_mamba2backbone_pa_t_kernel(
         const = ctx.enter_context(tc.tile_pool(name="const", bufs=1))
         inputs = ctx.enter_context(tc.tile_pool(name="inputs", bufs=N_GROUPS))
         per_group = ctx.enter_context(tc.tile_pool(name="per_group", bufs=3))
+        outputs = ctx.enter_context(tc.tile_pool(name="outputs", bufs=6))
         per_tile = ctx.enter_context(tc.tile_pool(name="per_tile", bufs=2 * MAX_TILES))
         psum_u = ctx.enter_context(tc.psum_pool(name="psum_u", bufs=2))
         psum_h = ctx.enter_context(tc.psum_pool(name="psum_h", bufs=H_BANKS))
@@ -292,7 +293,7 @@ def tile_mamba2backbone_pa_t_kernel(
         def add_bias_and_store(g):
             if not is_group(g):
                 return
-            o_rows = per_group.tile([P, GROUP_TILES[g], DETER], F32)
+            o_rows = outputs.tile([P, GROUP_TILES[g], DETER], F32)
             nc.vector.tensor_tensor(
                 out=o_rows[:],
                 in0=held["o_bank", g][:],
@@ -308,7 +309,7 @@ def tile_mamba2backbone_pa_t_kernel(
             for j in range(max(tiles, H_BANKS)):
                 if j < tiles:
                     add_bias_and_square(s, j)
-                    if s < 2:
+                    if s < 3:
                         first_matmuls(FIRST_TILE[s] + j + 1)
                     elif j + H_BANKS < tiles:
                         first_matmul(s, j + H_BANKS)
@@ -320,7 +321,7 @@ def tile_mamba2backbone_pa_t_kernel(
                         quantise("u", s + 1)
                     if s == -1:
                         spread_b1()
-                    if s < 2:
+                    if s < 3:
                         first_matmuls(FIRST_TILE[s] + j + 1 if tiles else 0)
                     if s == -1:
                         quantise("u", 1)
@@ -333,7 +334,7 @@ def tile_mamba2backbone_pa_t_kernel(
             if s == -1:
                 spread_norm_and_b2()
             for j in range(MAX_TILES):
-                if j % 2 == 0 and s >= 2:
+                if j % 2 == 0 and s >= 3:
                     first_matmul(s + 1, j // 2, times=TIMES)
                 normalise_transpose_silu(s - 1, j)
             if s < N_GROUPS:

@@ -125,6 +125,7 @@ def tile_mamba2backbone_pa_t_kernel(
         b1_sorted = const.tile([P, PACK, P], F32)
         nw_sorted = const.tile([P, PACK, P], F32)
         b2_spread = const.tile([P, DETER], F32)
+        b2_column = const.tile([P, 1], F32)
 
         def spread(row, width):
             z_bank = psum_z.tile([P, HIDDEN], F32)
@@ -139,7 +140,11 @@ def tile_mamba2backbone_pa_t_kernel(
             nw_bank = spread(nw_row, HIDDEN)
             b2_bank = spread(b2_row, DETER)
             nc.scalar.copy(out=nw_sorted[:], in_=nw_bank[:].rearrange("p (q t) -> p t q", t=PACK))
+            nc.tensor.matmul(
+                out=b2_bank[:, DETER : DETER + 1], lhsT=b2_row[:], rhs=ones[:, 0:1], start=True, stop=True
+            )
             nc.scalar.copy(out=b2_spread[:], in_=b2_bank[:, 0:DETER])
+            nc.scalar.copy(out=b2_column[:], in_=b2_bank[:, DETER : DETER + 1])
 
         def is_group(g):
             return 0 <= g < N_GROUPS
@@ -270,10 +275,48 @@ def tile_mamba2backbone_pa_t_kernel(
                 func=ACT.Silu,
             )
 
+        def on_scalar(g):
+            return 3 <= g < N_GROUPS - 4 and g % 3 == 0
+
+        def second_matmul_turned(g):
+            o_bank = psum_o.tile([P, GROUP_TILES[g] * P], F32, name="o_bank")
+            nc.tensor.matmul_mx(
+                out=o_bank[:],
+                lhsT=w2_words[:].bitcast(FP8X4),
+                lhsT_scale=w2_plane[:],
+                rhs=held["g_codes", g][:].bitcast(FP8X4),
+                rhs_scale=held["g_scales", g][:],
+                start=True,
+                stop=True,
+            )
+            held["o_bank", g] = o_bank
+
+        def add_bias_on_scalar(g):
+            if is_group(g) and on_scalar(g):
+                o_turned = outputs.tile([P, GROUP_TILES[g], P], F32)
+                nc.scalar.activation(out=o_turned[:], in_=held["o_bank", g][:].rearrange("p (j w) -> p j w", w=P), func=ACT.Identity, bias=b2_column[:])
+                held["o_turned", g] = o_turned
+
+        def turn_back(g):
+            if is_group(g) and on_scalar(g):
+                o_bank = psum_o.tile([P, GROUP_TILES[g], DETER], F32, name="o_bank")
+                for j in range(GROUP_TILES[g]):
+                    nc.tensor.transpose(o_bank[:, j, :], held["o_turned", g][:, j, :], identity[:])
+                held["o_bank", g] = o_bank
+
+        def store_from_scalar(g):
+            if is_group(g) and on_scalar(g):
+                o_rows = outputs.tile([P, GROUP_TILES[g], DETER], F32)
+                nc.scalar.copy(out=o_rows[:], in_=held["o_bank", g][:])
+                nc.sync.dma_start(out=group_rows(out, g), in_=o_rows[:])
+
         def second_matmul(g):
             if not is_group(g):
                 return
-            if g == N_GROUPS - 1:
+            if on_scalar(g):
+                second_matmul_turned(g)
+                return
+            if g >= N_GROUPS - 2:
                 o_bank = psum_h.tile([P, GROUP_TILES[g], DETER], F32, name="o_bank_last", tag="h_bank")
             else:
                 o_bank = psum_o.tile([P, GROUP_TILES[g], DETER], F32, name="o_bank")
@@ -291,7 +334,7 @@ def tile_mamba2backbone_pa_t_kernel(
             held["o_bank", g] = o_bank
 
         def add_bias_and_store(g):
-            if not is_group(g):
+            if not is_group(g) or on_scalar(g):
                 return
             o_rows = outputs.tile([P, GROUP_TILES[g], DETER], F32)
             nc.vector.tensor_tensor(
@@ -303,6 +346,7 @@ def tile_mamba2backbone_pa_t_kernel(
             nc.sync.dma_start(out=group_rows(out, g), in_=o_rows[:])
 
         for s in range(-3, N_GROUPS + 3):
+            store_from_scalar(s - 4)
             if s != 0 and s >= -1:
                 copy_u(s + 2)
             tiles = GROUP_TILES[s] if is_group(s) else 0
@@ -315,7 +359,6 @@ def tile_mamba2backbone_pa_t_kernel(
                         first_matmul(s, j + H_BANKS)
                 if s == 0 and j == 0:
                     enter(2)
-                    copy_u(2)
                 if j == H_BANKS - 1:
                     if s != 0:
                         quantise("u", s + 1)
@@ -326,18 +369,25 @@ def tile_mamba2backbone_pa_t_kernel(
                     if s == -1:
                         quantise("u", 1)
                     second_matmul(s - 3)
+                    if s == 0:
+                        copy_u(2)
+                        spread_norm_and_b2()
                     if s < -1 or s >= 0:
                         enter(s + 3)
             inverse_rms(s)
+            add_bias_on_scalar(s - 3)
             if s == -2:
                 copy_u(0)
-            if s == -1:
-                spread_norm_and_b2()
             for j in range(MAX_TILES):
                 if j % 2 == 0 and s >= 3:
                     first_matmul(s + 1, j // 2, times=TIMES)
-                normalise_transpose_silu(s - 1, j)
-            if s < N_GROUPS:
+                if s != N_GROUPS:
+                    normalise_transpose_silu(s - 1, j)
+            turn_back(s - 3)
+            if s == N_GROUPS - 1:
+                for j in range(GROUP_TILES[s]):
+                    normalise_transpose_silu(s, j)
+            if s < N_GROUPS - 1:
                 add_bias_and_store(s - 3)
                 quantise("g", s - 2)
             else:

from contextlib import ExitStack

import concourse.mybir as mybir
from concourse.masks import make_identity

F32 = mybir.dt.float32
BF16 = mybir.dt.bfloat16
I32 = mybir.dt.int32
U32 = mybir.dt.uint32
U8 = mybir.dt.uint8
FP8X4 = mybir.dt.float8_e4m3fn_x4
ALU = mybir.AluOpType
ACT = mybir.ActivationFunctionType

P = 128
PACK = 4
TOKENS = 8192
STOCH = 384
ACT_DIM = 128
K1 = STOCH + ACT_DIM
HIDDEN = 512
DETER = 128
EPS = 1e-4

MAX_TILES = 4
GROUP_TILES = [2, 2, 2] + [MAX_TILES] * 14 + [2]
N_GROUPS = len(GROUP_TILES)
FIRST_TILE = [sum(GROUP_TILES[:g]) for g in range(N_GROUPS)]
TILE_LIST = [(g, j) for g in range(N_GROUPS) for j in range(GROUP_TILES[g])]
TIMES = 2
H_BANKS = 2

FLOPS = 2 * TOKENS * K1 * HIDDEN + 2 * TOKENS * HIDDEN * DETER


def tile_mamba2backbone_pa_t_kernel(
    tc,
    stoch,
    action,
    tok_w1_words,
    tok_w1_scales,
    tok_b1,
    tok_nw,
    tok_w2_words,
    tok_w2_scales,
    tok_b2,
    out,
):
    nc = tc.nc

    def group_rows(tensor, g):
        first = P * FIRST_TILE[g]
        return tensor[first : first + P * GROUP_TILES[g], :].rearrange("(p j) k -> p j k", j=GROUP_TILES[g])

    with ExitStack() as ctx:
        const = ctx.enter_context(tc.tile_pool(name="const", bufs=1))
        inputs = ctx.enter_context(tc.tile_pool(name="inputs", bufs=N_GROUPS))
        per_group = ctx.enter_context(tc.tile_pool(name="per_group", bufs=3))
        outputs = ctx.enter_context(tc.tile_pool(name="outputs", bufs=6))
        per_tile = ctx.enter_context(tc.tile_pool(name="per_tile", bufs=2 * MAX_TILES))
        psum_u = ctx.enter_context(tc.psum_pool(name="psum_u", bufs=2))
        psum_h = ctx.enter_context(tc.psum_pool(name="psum_h", bufs=H_BANKS))
        psum_z = ctx.enter_context(tc.psum_pool(name="psum_z", bufs=3))
        psum_o = ctx.enter_context(tc.psum_pool(name="psum_o", bufs=1))
        ctx.enter_context(tc.manual_schedule())

        held = {}

        def load_group(g):
            u_rows = inputs.tile([P, GROUP_TILES[g], K1], BF16)
            nc.sync.dma_start(out=u_rows[:, :, STOCH:K1], in_=group_rows(action, g))
            nc.sync.dma_start(out=u_rows[:, :, 0:STOCH], in_=group_rows(stoch, g))
            held["u_rows", g] = u_rows

        def load_weight(words_dram, scales_dram, words, plane):
            nc.sync.dma_start(
                out=words[:].bitcast(I32),
                in_=words_dram[0].rearrange("p n t -> p (n t)").bitcast(I32),
            )
            for quadrant in range(4):
                nc.sync.dma_start(
                    out=plane[32 * quadrant : 32 * quadrant + 4, :].bitcast(I32),
                    in_=scales_dram[0, 4 * quadrant : 4 * quadrant + 4, :].bitcast(I32),
                )

        w1_words = const.tile([P, PACK * HIDDEN], U8, align_bytes=64)
        w1_plane = const.tile([P, HIDDEN], U8, align_bytes=64)
        w2_words = const.tile([P, PACK * DETER], U8, align_bytes=64)
        w2_plane = const.tile([P, DETER], U8, align_bytes=64)
        nc.vector.memset(w1_plane[:].bitcast(I32), 0)

        def row_of_zeros(width, name):
            rows = const.tile([P, width], BF16, name=name)
            nc.vector.memset(rows[:], 0.0)
            return rows

        b1_row = row_of_zeros(HIDDEN, "b1_row")
        nw_row = row_of_zeros(HIDDEN, "nw_row")
        b2_row = row_of_zeros(DETER, "b2_row")
        ones = const.tile([P, P], BF16)
        nc.vector.memset(ones[:], 1.0)

        load_group(0)
        load_weight(tok_w1_words, tok_w1_scales, w1_words, w1_plane)
        nc.sync.dma_start(out=b1_row[0:1, :], in_=tok_b1.unsqueeze(0))
        load_group(1)
        nc.sync.dma_start(out=nw_row[0:1, :], in_=tok_nw.unsqueeze(0))
        nc.sync.dma_start(out=b2_row[0:1, :], in_=tok_b2.unsqueeze(0))
        load_group(2)
        load_group(3)
        nc.vector.memset(w2_plane[:].bitcast(I32), 0)
        load_weight(tok_w2_words, tok_w2_scales, w2_words, w2_plane)
        for g in range(4, N_GROUPS):
            load_group(g)

        warm = const.tile([P, 1], F32)
        nc.vector.memset(warm[:], 0.0)
        nc.scalar.activation(out=warm[:], in_=warm[:], func=ACT.Silu)

        identity = const.tile([P, P], F32)
        make_identity(nc, identity[:])
        minus_half = const.tile([P, MAX_TILES], F32)
        nc.gpsimd.memset(minus_half[:], -0.5)

        b1_sorted = const.tile([P, PACK, P], F32)
        nw_sorted = const.tile([P, PACK, P], F32)
        b2_spread = const.tile([P, DETER], F32)
        b2_column = const.tile([P, 1], F32)

        def spread(row, width):
            z_bank = psum_z.tile([P, HIDDEN], F32)
            nc.tensor.matmul(out=z_bank[:, 0:width], lhsT=ones[:], rhs=row[:], start=True, stop=True)
            return z_bank

        def spread_b1():
            b1_bank = spread(b1_row, HIDDEN)
            nc.vector.tensor_copy(out=b1_sorted[:], in_=b1_bank[:].rearrange("p (q t) -> p t q", t=PACK))

        def spread_norm_and_b2():
            nw_bank = spread(nw_row, HIDDEN)
            b2_bank = spread(b2_row, DETER)
            nc.scalar.copy(out=nw_sorted[:], in_=nw_bank[:].rearrange("p (q t) -> p t q", t=PACK))
            nc.tensor.matmul(
                out=b2_bank[:, DETER : DETER + 1], lhsT=b2_row[:], rhs=ones[:, 0:1], start=True, stop=True
            )
            nc.scalar.copy(out=b2_spread[:], in_=b2_bank[:, 0:DETER])
            nc.scalar.copy(out=b2_column[:], in_=b2_bank[:, DETER : DETER + 1])

        def is_group(g):
            return 0 <= g < N_GROUPS

        def is_tile(g, j):
            return is_group(g) and j < GROUP_TILES[g]

        def clamp_action(g):
            if is_group(g):
                an = held["u_rows", g][:, :, STOCH:K1]
                nc.vector.tensor_scalar(out=an, in0=an, scalar1=1.0, scalar2=-1.0, op0=ALU.min, op1=ALU.max)

        def transpose_u(g, j):
            if not is_tile(g, j):
                return
            if j % 2 == 0:
                u_bank = psum_u.tile([P, 2, 2, P], F32)
                held["u_bank", g, j // 2] = u_bank
            words = held["u_rows", g][:, j, :].bitcast(F32)
            for half in range(2):
                nc.tensor.transpose(
                    held["u_bank", g, j // 2][:, j % 2, half, :], words[:, half : K1 // 2 : 2], identity[:]
                )

        def enter(g):
            clamp_action(g)
            for j in range(MAX_TILES):
                transpose_u(g, j)

        def copy_u(g):
            if not is_group(g):
                return
            pairs = GROUP_TILES[g] // 2
            u_grouped = per_group.tile([P, PACK * P * GROUP_TILES[g]], BF16, align_bytes=64)
            as_words = u_grouped[:].bitcast(F32).rearrange("p (r i w h) -> p r i w h", r=pairs, i=2, h=2)
            for pair in range(pairs):
                nc.scalar.copy(
                    out=as_words[:, pair],
                    in_=held["u_bank", g, pair][:].rearrange("p i h w -> p i w h"),
                )
            held["u_grouped", g] = u_grouped

        def quantise(name, g):
            if not is_group(g):
                return
            codes = per_group.tile([P, P * GROUP_TILES[g]], U32, align_bytes=64, tag=name + "_codes")
            scales = per_group.tile([P, P * GROUP_TILES[g]], U8, align_bytes=64, tag=name + "_scales")
            nc.vector.quantize_mx(out=codes[:].bitcast(FP8X4), scales=scales[:], in_=held[name + "_grouped", g][:])
            held[name + "_codes", g] = codes
            held[name + "_scales", g] = scales

        def first_matmul(g, j, times=1):
            if not is_tile(g, j):
                return
            tokens = slice(P * j, P * (j + 1))
            h_bank = psum_h.tile([P, HIDDEN], F32)
            for repeat in range(times):
                nc.tensor.matmul_mx(
                    out=h_bank[:],
                    lhsT=held["u_codes", g][:, tokens].bitcast(FP8X4),
                    lhsT_scale=held["u_scales", g][:, tokens],
                    rhs=w1_words[:].bitcast(FP8X4),
                    rhs_scale=w1_plane[:],
                    start=True,
                    stop=True,
                )
            held["h_bank", g, j] = h_bank

        multiplied = []

        def first_matmuls(emptied):
            while len(multiplied) < min(emptied + H_BANKS, len(TILE_LIST)):
                g, j = TILE_LIST[len(multiplied)]
                if ("u_codes", g) not in held:
                    return
                first_matmul(g, j)
                multiplied.append((g, j))

        def add_bias_and_square(g, j):
            if j == 0:
                sum_sq = per_group.tile([P, GROUP_TILES[g]], F32)
                held["sum_sq", g] = sum_sq
            h_sorted = per_tile.tile([P, PACK, P], F32)
            nc.vector.tensor_tensor(
                out=h_sorted[:],
                in0=held["h_bank", g, j][:].rearrange("p (q t) -> p t q", t=PACK),
                in1=b1_sorted[:],
                op=ALU.add,
            )
            squares = per_tile.tile([P, PACK, P], BF16)
            nc.scalar.activation(
                out=squares[:], in_=h_sorted[:], func=ACT.Square, accum_out=held["sum_sq", g][:, j : j + 1]
            )
            held["h_sorted", g, j] = h_sorted

        def inverse_rms(g):
            if not is_group(g):
                return
            mean_sq = per_group.tile([P, GROUP_TILES[g]], F32)
            inv_rms = per_group.tile([P, GROUP_TILES[g]], F32)
            nc.gpsimd.tensor_scalar(
                out=mean_sq[:], in0=held["sum_sq", g][:], scalar1=1.0 / HIDDEN, scalar2=EPS, op0=ALU.mult, op1=ALU.add
            )
            nc.gpsimd.tensor_tensor(out=inv_rms[:], in0=mean_sq[:], in1=minus_half[:, 0 : GROUP_TILES[g]], op=ALU.pow)
            held["inv_rms", g] = inv_rms

        def normalise_transpose_silu(g, j):
            if not is_tile(g, j):
                return
            if j == 0:
                g_grouped = per_group.tile([P, PACK * P * GROUP_TILES[g]], BF16, align_bytes=64)
                held["g_grouped", g] = g_grouped
            z_sorted = per_tile.tile([P, PACK, P], F32)
            nc.vector.scalar_tensor_tensor(
                out=z_sorted[:],
                in0=held["h_sorted", g, j][:],
                scalar=held["inv_rms", g][:, j : j + 1],
                in1=nw_sorted[:],
                op0=ALU.mult,
                op1=ALU.mult,
            )
            z_bank = psum_z.tile([P, PACK, P], F32)
            for t in range(PACK):
                nc.tensor.transpose(z_bank[:, t, :], z_sorted[:, t, :], identity[:])
            nc.scalar.activation(
                out=held["g_grouped", g][:, PACK * P * j : PACK * P * (j + 1)].rearrange("p (w t) -> p w t", t=PACK),
                in_=z_bank[:].rearrange("p t w -> p w t"),
                func=ACT.Silu,
            )

        def on_scalar(g):
            return 3 <= g < N_GROUPS - 4 and g % 3 == 0

        def second_matmul_turned(g):
            o_bank = psum_o.tile([P, GROUP_TILES[g] * P], F32, name="o_bank")
            nc.tensor.matmul_mx(
                out=o_bank[:],
                lhsT=w2_words[:].bitcast(FP8X4),
                lhsT_scale=w2_plane[:],
                rhs=held["g_codes", g][:].bitcast(FP8X4),
                rhs_scale=held["g_scales", g][:],
                start=True,
                stop=True,
            )
            held["o_bank", g] = o_bank

        def add_bias_on_scalar(g):
            if is_group(g) and on_scalar(g):
                o_turned = outputs.tile([P, GROUP_TILES[g], P], F32)
                nc.scalar.activation(out=o_turned[:], in_=held["o_bank", g][:].rearrange("p (j w) -> p j w", w=P), func=ACT.Identity, bias=b2_column[:])
                held["o_turned", g] = o_turned

        def turn_back(g):
            if is_group(g) and on_scalar(g):
                o_bank = psum_o.tile([P, GROUP_TILES[g], DETER], F32, name="o_bank")
                for j in range(GROUP_TILES[g]):
                    nc.tensor.transpose(o_bank[:, j, :], held["o_turned", g][:, j, :], identity[:])
                held["o_bank", g] = o_bank

        def store_from_scalar(g):
            if is_group(g) and on_scalar(g):
                o_rows = outputs.tile([P, GROUP_TILES[g], DETER], F32)
                nc.scalar.copy(out=o_rows[:], in_=held["o_bank", g][:])
                nc.sync.dma_start(out=group_rows(out, g), in_=o_rows[:])

        def second_matmul(g):
            if not is_group(g):
                return
            if on_scalar(g):
                second_matmul_turned(g)
                return
            if g >= N_GROUPS - 2:
                o_bank = psum_h.tile([P, GROUP_TILES[g], DETER], F32, name="o_bank_last", tag="h_bank")
            else:
                o_bank = psum_o.tile([P, GROUP_TILES[g], DETER], F32, name="o_bank")
            for j in range(GROUP_TILES[g]):
                tokens = slice(P * j, P * (j + 1))
                nc.tensor.matmul_mx(
                    out=o_bank[:, j, :],
                    lhsT=held["g_codes", g][:, tokens].bitcast(FP8X4),
                    lhsT_scale=held["g_scales", g][:, tokens],
                    rhs=w2_words[:].bitcast(FP8X4),
                    rhs_scale=w2_plane[:],
                    start=True,
                    stop=True,
                )
            held["o_bank", g] = o_bank

        def add_bias_and_store(g):
            if not is_group(g) or on_scalar(g):
                return
            o_rows = outputs.tile([P, GROUP_TILES[g], DETER], F32)
            nc.vector.tensor_tensor(
                out=o_rows[:],
                in0=held["o_bank", g][:],
                in1=b2_spread[:].unsqueeze(1).to_broadcast([P, GROUP_TILES[g], DETER]),
                op=ALU.add,
            )
            nc.sync.dma_start(out=group_rows(out, g), in_=o_rows[:])

        for s in range(-3, N_GROUPS + 3):
            store_from_scalar(s - 4)
            if s != 0 and s >= -1:
                copy_u(s + 2)
            tiles = GROUP_TILES[s] if is_group(s) else 0
            for j in range(max(tiles, H_BANKS)):
                if j < tiles:
                    add_bias_and_square(s, j)
                    if s < 3:
                        first_matmuls(FIRST_TILE[s] + j + 1)
                    elif j + H_BANKS < tiles:
                        first_matmul(s, j + H_BANKS)
                if s == 0 and j == 0:
                    enter(2)
                if j == H_BANKS - 1:
                    if s != 0:
                        quantise("u", s + 1)
                    if s == -1:
                        spread_b1()
                    if s < 3:
                        first_matmuls(FIRST_TILE[s] + j + 1 if tiles else 0)
                    if s == -1:
                        quantise("u", 1)
                    second_matmul(s - 3)
                    if s == 0:
                        copy_u(2)
                        spread_norm_and_b2()
                    if s < -1 or s >= 0:
                        enter(s + 3)
            inverse_rms(s)
            add_bias_on_scalar(s - 3)
            if s == -2:
                copy_u(0)
            for j in range(MAX_TILES):
                if j % 2 == 0 and s >= 3:
                    first_matmul(s + 1, j // 2, times=TIMES)
                if s != N_GROUPS:
                    normalise_transpose_silu(s - 1, j)
            turn_back(s - 3)
            if s == N_GROUPS - 1:
                for j in range(GROUP_TILES[s]):
                    normalise_transpose_silu(s, j)
            if s < N_GROUPS - 1:
                add_bias_and_store(s - 3)
                quantise("g", s - 2)
            else:
                quantise("g", s - 2)
                add_bias_and_store(s - 3)
